import numpy as np
import ml_dtypes


def mxq(x, axis, fmt="e4m3"):
    dtype, down = {"e4m3": (ml_dtypes.float8_e4m3fn, 7), "e5m2": (ml_dtypes.float8_e5m2, 14)}[fmt]
    v = np.moveaxis(np.asarray(x, np.float32).astype(ml_dtypes.bfloat16).astype(np.float64), axis, -1)
    blocks = v.reshape(v.shape[:-1] + (-1, 32))
    amax = np.abs(blocks).max(-1, keepdims=True)
    byte = np.maximum(np.where(amax > 0, np.frexp(amax)[1] - 1 + 127, 0) - down, 1)
    scale = np.exp2(byte - 127.0)
    codes = (blocks / scale).astype(np.float32).astype(dtype).astype(np.float64)
    return np.moveaxis((codes * scale).reshape(v.shape), -1, axis)


WIDE = False


def mx_kscale(k):
    if not WIDE:
        return np.ones(k)
    levels = np.array([30, -30])
    if k % 512:
        return np.exp2(np.random.permutation(np.resize(levels, k // 32))).repeat(32)
    a = np.empty((k // 512, 16))
    for p in range(k // 512):
        a[p, :8] = np.random.permutation(np.resize(levels, 8))
        for g in range(8):
            far = levels[np.abs(levels - a[p, g]) >= 10]
            a[p, g + 8] = far[np.random.randint(len(far))]
    return np.exp2(a.ravel()).repeat(32)


BF16 = ml_dtypes.bfloat16


def bf(x):
    return np.asarray(x, np.float32).astype(BF16)


def f64(x):
    return np.asarray(x).astype(np.float64)


B, S, HID, NQ, NG, D, OFF = 1, 512, 2048, 16, 4, 128, 512
NKV = NQ // NG
HALF = D // 2


def rope(u, cos, sin):
    b, s, h, d = u.shape
    up = u.reshape(b, s, h, HALF, 2)
    ur, ui = up[..., 0], up[..., 1]
    c = cos[None, :, None, :]
    sn = sin[None, :, None, :]
    return np.stack([ur * c - ui * sn, ur * sn + ui * c], axis=-1).reshape(b, s, h, d)


def setup_inputs():
    sc = mx_kscale(HID)
    r = 1.0 / np.sqrt(HID)
    return {
        "x": bf(np.random.standard_normal((B, S, HID)) * sc),
        "precomp_freqs_cos": bf(np.random.uniform(-1.0, 1.0, (S, HALF))),
        "precomp_freqs_sin": bf(np.random.uniform(-1.0, 1.0, (S, HALF))),
        "q_w": bf(np.random.standard_normal((NQ * D, HID)) * 2.0 * r / sc),
        "q_b": bf(np.random.standard_normal(NQ * D) * 0.5),
        "k_w": bf(np.random.standard_normal((NKV * D, HID)) * 1.2 * r / sc),
        "k_b": bf(np.random.standard_normal(NKV * D) * 0.3),
        "v_w": bf(np.random.standard_normal((NKV * D, HID)) * r / sc),
        "v_b": bf(np.random.standard_normal(NKV * D) * 0.3),
    }


def reference(x, precomp_freqs_cos, precomp_freqs_sin, q_w, q_b, k_w, k_b, v_w, v_b):
    xq = mxq(f64(x), 2, "e5m2")
    q = ((xq @ mxq(f64(q_w), 1, "e4m3").T) + f64(q_b)).reshape(B, S, NQ, D)
    k = ((xq @ mxq(f64(k_w), 1, "e4m3").T) + f64(k_b)).reshape(B, S, NKV, D)
    v = ((xq @ mxq(f64(v_w), 1, "e4m3").T) + f64(v_b)).reshape(B, S, NKV, D)
    cos, sin = f64(precomp_freqs_cos), f64(precomp_freqs_sin)
    return rope(q, cos, sin), rope(k, cos, sin), v

from contextlib import ExitStack

import concourse.mybir as mybir
from concourse.masks import make_identity

S, HID, NQ, NKV, D = 512, 2048, 16, 4, 128
FLOPS = 2 * S * HID * (NQ + 2 * NKV) * D

F32 = mybir.dt.float32
BF16 = mybir.dt.bfloat16
U32 = mybir.dt.uint32
U8 = mybir.dt.uint8
E4M3X4 = mybir.dt.float8_e4m3fn_x4
E5M2X4 = mybir.dt.float8_e5m2_x4
ADD = mybir.AluOpType.add
MULT = mybir.AluOpType.mult
COPY = mybir.ActivationFunctionType.Copy

P = 128
TT = S // P
PASSES = HID // 512
QG = 4
PAIRS = D // 2
GROUPS = [("k", 0)] + [("q", g) for g in range(QG)] + [("k", 1), ("v", 0)]
HEAD_BANKS = 8
PLAN = [(1, 4), (1, 4), (1, 4), (1, 2)] + [(2, 4)] * 8 + [(2, 2)] + [(2, 0)] * 3
W_AHEAD = 12
FIRST_LOADS = 2
BIAS_AFTER = {1: 2, 7: 0, 11: 1}
SORT_ON_SCALAR = []
SORT_ON_VECTOR = []


def tile_attention_pa_kernel(tc, x, cos, sin, q_w, q_b, k_w, k_b, v_w, v_b, out_q, out_k, out_v):
    nc = tc.nc
    x_rows = x.rearrange("b (p t) k -> (b t) p k", t=TT)
    q_rows = q_w.rearrange("(p g jj e) k -> g jj p e k", g=QG, jj=2, e=2)
    k_rows = k_w.rearrange("(jj p e) k -> jj p e k", jj=2, e=2)
    v_rows = v_w.rearrange("(jj p e) k -> jj p e k", jj=2, e=2)
    oq = out_q.rearrange("b (p t) h d -> (b t) p (h d)", t=TT)
    ok = out_k.rearrange("b (p t) h d -> (b t) p (h d)", t=TT)
    ov = out_v.rearrange("b (p t) h d -> (b t) p (h d)", t=TT)

    with ExitStack() as ctx:
        keep = ctx.enter_context(tc.tile_pool(name="keep", bufs=1))
        work = ctx.enter_context(tc.tile_pool(name="work", bufs=3))
        psum = ctx.enter_context(tc.psum_pool(name="psum", bufs=4))
        ctx.enter_context(tc.manual_schedule())

        def w_banks(kind, g):
            if kind == "k":
                return [(kind, g, c, g) for c in range(PASSES)]
            return [(kind, g, c, jj) for c in range(PASSES) for jj in range(2)]

        banks = [("x", 0, 0), ("x", 0, 1)] + w_banks(*GROUPS[0])
        banks += [("x", t, half) for t in range(1, TT) for half in range(2)]
        for group in GROUPS[1:]:
            banks += w_banks(*group)
        order = list(banks)

        def chunk_of(bank):
            return bank if bank[0] == "x" else (bank[0], bank[1], bank[2] // 2, bank[3])

        chunks = []
        for bank in banks:
            if chunk_of(bank) not in chunks:
                chunks.append(chunk_of(bank))
        raw = {}

        def load(chunk):
            if chunk[0] == "x":
                t, half = chunk[1:]
                tile = work.tile([P, 1024], BF16, name="x_raw", tag="x_raw", bufs=2 * TT)
                nc.sync.dma_start(out=tile[:], in_=x_rows[t][:, 1024 * half : 1024 * (half + 1)])
            else:
                kind, g, half, jj = chunk
                rows = q_rows[g, jj] if kind == "q" else k_rows[jj] if kind == "k" else v_rows[jj]
                tile = work.tile([P, 2, 1024], BF16, name="w_raw", tag="w_raw", bufs=W_AHEAD)
                nc.sync.dma_start(out=tile[:], in_=rows[:, :, 1024 * half : 1024 * (half + 1)])
            raw[chunk] = tile

        bias_rows = keep.tile([P, 512], BF16, name="bias_rows")
        nc.vector.memset(bias_rows[:], 0.0)
        ident = keep.tile([P, P], F32, name="ident")
        make_identity(nc, ident[:])
        ident_bf = keep.tile([P, P], BF16, name="ident_bf")
        nc.scalar.activation(out=ident_bf[:], in_=ident[:], func=COPY)
        sign = keep.tile([P, 2], F32, name="sign")
        nc.vector.memset(sign[:, 0:1], -1.0)
        nc.vector.memset(sign[:, 1:2], 1.0)

        to_load = list(chunks)
        for i in range(FIRST_LOADS):
            load(to_load.pop(0))
        nc.sync.dma_start(out=bias_rows[0:4, :], in_=q_b.rearrange("(r n) -> r n", r=4))
        nc.sync.dma_start(out=bias_rows[4:5, :], in_=k_b.rearrange("(r n) -> r n", r=1))
        nc.sync.dma_start(out=bias_rows[5:6, :], in_=v_b.rearrange("(r n) -> r n", r=1))
        cos_raw = keep.tile([P, TT * PAIRS], BF16, name="cos_raw")
        sin_raw = keep.tile([P, TT * PAIRS], BF16, name="sin_raw")
        for i in range(FIRST_LOADS, FIRST_LOADS + 2):
            load(to_load.pop(0))
        nc.sync.dma_start(out=cos_raw[:], in_=cos.rearrange("(p t) j -> p (t j)", t=TT))
        nc.sync.dma_start(out=sin_raw[:], in_=sin.rearrange("(p t) j -> p (t j)", t=TT))
        for i in range(FIRST_LOADS + 2, 2 * TT + W_AHEAD):
            load(to_load.pop(0))
        cos2 = keep.tile([P, TT * PAIRS, 2], F32, name="cos2")
        sin2 = keep.tile([P, TT * PAIRS, 2], F32, name="sin2")

        def widen_tables():
            nc.vector.tensor_copy(out=cos2[:], in_=cos_raw[:].unsqueeze(2).to_broadcast([P, TT * PAIRS, 2]))
            nc.vector.tensor_tensor(
                out=sin2[:],
                in0=sin_raw[:].unsqueeze(2).to_broadcast([P, TT * PAIRS, 2]),
                in1=sign[:].unsqueeze(1).to_broadcast([P, TT * PAIRS, 2]),
                op=MULT,
            )

        bias = keep.tile([P, 6 * 512], BF16, name="bias")

        def spread_bias(i):
            both = psum.tile([P, 1024], BF16, name="both", tag="acc")
            for r in (2 * i, 2 * i + 1):
                nc.tensor.matmul(
                    out=both[:, 512 * (r % 2) : 512 * (r % 2 + 1)],
                    lhsT=ident_bf[:, r : r + 1].to_broadcast([P, P]),
                    rhs=bias_rows[:],
                    start=True,
                    stop=True,
                )
            nc.scalar.copy(out=bias[:, 1024 * i : 1024 * (i + 1)], in_=both[:])

        grouped = {}
        codes = {}
        to_quantise = []
        sorted_words = {}

        def words_of(bank):
            words = raw[chunk_of(bank)][:].bitcast(F32)
            if bank[0] == "x":
                return words.rearrange("p (a w) -> p a w", a=2)
            return words[:, :, 256 * (bank[2] % 2) : 256 * (bank[2] % 2 + 1)]

        def sort_words(bank):
            tile = work.tile([P, 2, 2, P], F32, name="sorted", tag="sorted", bufs=6)
            copy = nc.scalar.copy if order.index(bank) in SORT_ON_SCALAR else nc.vector.tensor_copy
            copy(out=tile[:], in_=words_of(bank).rearrange("p a (i u) -> p a u i", u=2))
            sorted_words[bank] = tile

        def sort_ahead(count):
            for bank in banks[:count]:
                if order.index(bank) in SORT_ON_SCALAR + SORT_ON_VECTOR and bank not in sorted_words:
                    sort_words(bank)

        def transpose_bank(bank):
            turned = psum.tile([P, 4, P], F32, name="turned", tag="turned")
            words = words_of(bank)
            for a in range(2):
                for u in range(2):
                    source = sorted_words[bank][:, a, u, :] if bank in sorted_words else words[:, a, u::2]
                    nc.tensor.transpose(turned[:, 2 * a + u, :], source, ident[:])
            if bank[0] == "x":
                tile = work.tile([P, 2, P, 2], F32, name="half_grouped", tag="half_grouped", bufs=3, align_bytes=64)
                nc.scalar.copy(out=tile[:], in_=turned[:].rearrange("p (g u) r -> p g r u", u=2))
                grouped[bank] = tile[:].rearrange("p g r u -> p (g r u)")
                to_quantise.append(bank)
                return
            kind, g, c, jj = bank
            key = (kind, g, c)
            if kind == "k":
                tile = work.tile([P, P, 4], F32, name="half_grouped", tag="half_grouped", bufs=3, align_bytes=64)
                nc.scalar.copy(out=tile[:], in_=turned[:].rearrange("p eu r -> p r eu"))
                grouped[key] = tile[:].rearrange("p r eu -> p (r eu)")
                to_quantise.append(key)
            else:
                if jj == 0:
                    grouped[key] = work.tile([P, 1024], F32, name="w_grouped", tag="w_grouped", bufs=4, align_bytes=64)[:]
                pattern = "p (r jj eu) -> p jj r eu" if kind == "q" else "p (jj r eu) -> p jj r eu"
                nc.scalar.copy(out=grouped[key].rearrange(pattern, jj=2, eu=4)[:, jj], in_=turned[:].rearrange("p eu r -> p r eu"))
                if jj == 1:
                    to_quantise.append(key)
            if c % 2 == 1 and to_load:
                load(to_load.pop(0))

        def quantise_ready():
            while to_quantise:
                key = to_quantise.pop(0)
                width = grouped[key].shape[1] // 2
                tag, fmt, bufs = ("x", E5M2X4, 2 * TT) if key[0] == "x" else ("w", E4M3X4, 12)
                packed = work.tile([P, width], U32, name=tag + "_codes", tag=tag + "_codes", bufs=bufs, align_bytes=64)
                scales = work.tile([P, width], U8, name=tag + "_scales", tag=tag + "_scales", bufs=bufs, align_bytes=64)
                nc.vector.quantize_mx(out=packed[:].bitcast(fmt), scales=scales[:], in_=grouped[key].bitcast(BF16))
                codes[key] = (packed, scales)

        jobs = [(kind, g, t) for kind, g in GROUPS for t in range(TT)]
        acc, summed, by_cos, by_sin = {}, {}, {}, {}
        q_out = [keep.tile([P, NQ * D], F32, name="q_out%d" % t) for t in range(TT)]

        def width_of(job):
            return 256 if job[0] == "k" else 512

        def multiply(job):
            kind, g, t = job
            acc[job] = psum.tile([P, width_of(job)], F32, name="acc", tag="acc")
            for c in range(PASSES):
                x_codes, x_scales = codes[("x", t, c // 2)]
                w_codes, w_scales = codes[(kind, g, c)]
                cols = slice(P * (c % 2), P * (c % 2 + 1))
                nc.tensor.matmul_mx(
                    out=acc[job][:],
                    lhsT=x_codes[:, cols].bitcast(E5M2X4),
                    lhsT_scale=x_scales[:, cols],
                    rhs=w_codes[:].bitcast(E4M3X4),
                    rhs_scale=w_scales[:],
                    start=(c == 0),
                    stop=(c == PASSES - 1),
                )

        def add_bias(job):
            kind, g, t = job
            width = width_of(job)
            if kind == "q":
                row = bias[:, 0 : NQ * D].rearrange("p (r g c) -> p r g c", g=QG, c=4)[:, :, g, :]
            else:
                first = NQ * D + (width * g if kind == "k" else NKV * D)
                row = bias[:, first : first + width].rearrange("p (r c) -> p r c", c=4)
            tag, bufs = ("kv_out", 8) if kind == "v" else ("summed", 4)
            summed[job] = work.tile([P, width // 4, 4], F32, name=tag, tag=tag, bufs=bufs)
            nc.vector.tensor_tensor(out=summed[job][:], in0=acc[job][:].rearrange("p (r c) -> p r c", c=4), in1=row, op=ADD)
            if kind == "v":
                nc.sync.dma_start(out=ov[t], in_=summed[job][:].rearrange("p r c -> p (r c)"))

        def table(tab, job):
            kind, g, t = job
            mine = tab[:, PAIRS * t : PAIRS * (t + 1), :]
            if kind == "q":
                return mine.rearrange("p (m g jj) e -> p m g jj e", g=QG, jj=2)[:, :, g].unsqueeze(1).to_broadcast([P, NQ, 8, 2, 2])
            return mine.rearrange("p (m jj) e -> p m jj e", jj=2).unsqueeze(1).to_broadcast([P, 2, 32, 2, 2])

        def products(job):
            kind, g, t = job
            if kind == "v":
                return
            heads = NQ if kind == "q" else 2
            runs = width_of(job) // 4
            u = summed[job][:].rearrange("p (h m) (jj e) -> p h m jj e", h=heads, e=2)
            by_sin[job] = work.tile([P, runs, 4], F32, name="by_sin", tag="by_sin", bufs=4)
            view = by_sin[job][:].rearrange("p (h m) (jj e) -> p h m jj e", h=heads, e=2)
            nc.vector.tensor_tensor(out=view, in0=u[:, :, :, :, ::-1], in1=table(sin2, job), op=MULT)
            if kind == "k":
                by_cos[job] = work.tile([P, runs, 4], F32, name="by_cos", tag="by_cos", bufs=4)
                view = by_cos[job][:].rearrange("p (h m) (jj e) -> p h m jj e", h=heads, e=2)
                nc.vector.tensor_tensor(out=view, in0=u, in1=table(cos2, job), op=MULT)

        def finish(job):
            kind, g, t = job
            if kind == "v":
                return
            if kind == "k":
                done = work.tile([P, 64, 4], F32, name="kv_out", tag="kv_out", bufs=8)
                nc.vector.tensor_tensor(out=done[:], in0=by_cos[job][:], in1=by_sin[job][:], op=ADD)
                stores.append((ok[t][:, 256 * g : 256 * (g + 1)], done[:].rearrange("p r c -> p (r c)")))
                flush_stores()
                return
            u = summed[job][:].rearrange("p (h m) (jj e) -> p m jj h e", h=NQ, e=2)
            by_pair = work.tile([P, 8, 2, NQ, 2], F32, name="by_cos", tag="by_cos", bufs=4)
            for m in range(8):
                for jj in range(2):
                    j = PAIRS * t + 8 * m + 2 * g + jj
                    nc.scalar.activation(out=by_pair[:, m, jj], in_=u[:, m, jj], func=COPY, scale=cos2[:, j, 0:1])
            nc.vector.tensor_tensor(
                out=q_out[t][:].rearrange("p (h m g jj e) -> p h m g jj e", h=NQ, g=QG, jj=2, e=2)[:, :, :, g],
                in0=by_pair[:].rearrange("p m jj h e -> p h m jj e"),
                in1=by_sin[job][:].rearrange("p (h m) (jj e) -> p h m jj e", h=NQ, e=2),
                op=ADD,
            )
            if g == QG - 1:
                nc.sync.dma_start(out=oq[t], in_=q_out[t][:])

        stores = []

        def flush_stores():
            while stores and not to_load:
                target, source = stores.pop(0)
                nc.sync.dma_start(out=target, in_=source)

        def next_bank():
            bank = banks.pop(0)
            transpose_bank(bank)
            i = order.index(bank)
            if i in BIAS_AFTER:
                spread_bias(BIAS_AFTER[i])
            flush_stores()

        for i in range(HEAD_BANKS):
            sort_ahead(2)
            quantise_ready()
            next_bank()
            if i == 5:
                widen_tables()
        quantise_ready()
        waiting = []
        for products_here, banks_here in PLAN:
            earlier, waiting = waiting, []
            sort_ahead(banks_here)
            for i in range(products_here):
                job = jobs.pop(0)
                multiply(job)
                quantise_ready()
                add_bias(job)
                if i > 0:
                    products(waiting[-1])
                if earlier:
                    finish(earlier.pop(0))
                waiting.append(job)
            while earlier:
                finish(earlier.pop(0))
            for i in range(banks_here):
                next_bank()
                if i == 1:
                    quantise_ready()
            products(waiting[-1])
        for job in waiting:
            finish(job)
